import numpy as np
import ml_dtypes


def mxq(x, axis, fmt="e4m3"):
    dtype, down = {"e4m3": (ml_dtypes.float8_e4m3fn, 7), "e5m2": (ml_dtypes.float8_e5m2, 14)}[fmt]
    v = np.moveaxis(np.asarray(x, np.float32).astype(ml_dtypes.bfloat16).astype(np.float64), axis, -1)
    blocks = v.reshape(v.shape[:-1] + (-1, 32))
    amax = np.abs(blocks).max(-1, keepdims=True)
    byte = np.maximum(np.where(amax > 0, np.frexp(amax)[1] - 1 + 127, 0) - down, 1)
    scale = np.exp2(byte - 127.0)
    codes = (blocks / scale).astype(np.float32).astype(dtype).astype(np.float64)
    return np.moveaxis((codes * scale).reshape(v.shape), -1, axis)


WIDE = False


def mx_kscale(k):
    if not WIDE:
        return np.ones(k)
    levels = np.array([10, -10, 5, -5, 0])
    a = np.random.permutation(np.resize(levels, k // 512 * 4)).reshape(k // 512, 4)
    idx = np.arange(k)
    return np.exp2(a[idx // 512, idx % 128 // 32])


BF16 = ml_dtypes.bfloat16


def bf(x):
    return np.asarray(x, np.float32).astype(BF16)


def f64(x):
    return np.asarray(x).astype(np.float64)


E2M1 = np.array([0.0, 0.5, 1.0, 1.5, 2.0, 3.0, 4.0, 6.0, -0.0, -0.5, -1.0, -1.5, -2.0, -3.0, -4.0, -6.0])


def pack_weight(w, fmt):
    k, n = w.shape
    w = f64(bf(w)).reshape(k // 32, 32, n)
    amax = np.abs(w).max(1)
    if fmt == "e4m3":
        byte = np.frexp(amax)[1] - 1 + 127 - 7
    else:
        mant, ex = np.frexp(amax / 6.0)
        byte = np.where(mant > 0.5, ex, ex - 1) + 127
    byte = np.clip(np.where(amax > 0, byte, 1), 1, 254)
    scaled = (w * np.exp2(127.0 - byte)[:, None, :]).reshape(k, n).astype(np.float32)
    by_word = np.ascontiguousarray(scaled.reshape(k // 512, 128, 4, n).transpose(0, 1, 3, 2))
    if fmt == "e4m3":
        words = by_word.astype(ml_dtypes.float8_e4m3fn).view(np.uint8)
    else:
        c = by_word.astype(ml_dtypes.float4_e2m1fn).view(np.uint8) & 0xF
        words = c[..., 0::2] | (c[..., 1::2] << 4)
    return np.ascontiguousarray(words), np.ascontiguousarray(byte.astype(np.uint8).reshape(k // 512, 16, n))


def unpack_weight(words, scales, fmt):
    g, p, n, _ = words.shape
    if fmt == "e4m3":
        vals = np.ascontiguousarray(words).view(ml_dtypes.float8_e4m3fn).astype(np.float64)
    else:
        nib = np.empty((g, p, n, 4), np.uint8)
        nib[..., 0::2] = words & 0xF
        nib[..., 1::2] = words >> 4
        vals = E2M1[nib]
    vals = vals * np.repeat(np.exp2(scales.astype(np.float64) - 127.0), 8, axis=1)[..., None]
    return vals.transpose(0, 1, 3, 2).reshape(g * 512, n)

def pack4(w):
    words, scales = pack_weight(w, "e2m1")
    return words.reshape(words.shape[0], 128, -1), scales


def unpack4(words, scales):
    return unpack_weight(words.reshape(words.shape[0], 128, -1, 2), scales, "e2m1")


B, S, D, H, HKV, HD, WINDOW, KB = 1, 512, 2048, 16, 8, 128, 256, 512
EPS = 1e-6
THETA = 10000.0


def rope_tables():
    inv_freq = 1.0 / THETA ** (np.arange(0, HD, 2) / HD)
    ang = np.arange(S)[:, None] * inv_freq[None, :]
    emb = np.concatenate([ang, ang], axis=-1)
    return np.broadcast_to(np.cos(emb)[None], (B, S, HD)), np.broadcast_to(np.sin(emb)[None], (B, S, HD))


def rms_norm(x, gain):
    var = np.mean(x * x, axis=-1, keepdims=True)
    return x * (1.0 / np.sqrt(var + EPS)) * gain


def rotate_half(x):
    return np.concatenate([-x[..., HD // 2:], x[..., :HD // 2]], axis=-1)


def apply_rope(x, cos, sin):
    return x * cos[:, :, None, :] + rotate_half(x) * sin[:, :, None, :]


def setup_inputs():
    s = mx_kscale(D)
    cos, sin = rope_tables()
    hidden_states = bf(np.random.standard_normal((B, S, D)) * s)
    Wq_words, Wq_scales = pack4(np.random.standard_normal((D, H * HD)) / np.sqrt(D) / s[:, None])
    Wk_words, Wk_scales = pack4(np.random.standard_normal((D, HKV * HD)) / np.sqrt(D) / s[:, None])
    Wv_words, Wv_scales = pack4(np.random.standard_normal((D, HKV * HD)) * 2.0 / np.sqrt(D) / s[:, None])
    q_scale = bf(np.random.uniform(0.5, 1.5, HD))
    k_scale = bf(np.random.uniform(0.5, 1.5, HD))
    return {
        "hidden_states": hidden_states,
        "cos": bf(cos),
        "sin": bf(sin),
        "Wq_words": Wq_words,
        "Wq_scales": Wq_scales,
        "Wk_words": Wk_words,
        "Wk_scales": Wk_scales,
        "Wv_words": Wv_words,
        "Wv_scales": Wv_scales,
        "q_scale": q_scale,
        "k_scale": k_scale,
    }


def reference(hidden_states, cos, sin, Wq_words, Wq_scales, Wk_words, Wk_scales, Wv_words, Wv_scales, q_scale, k_scale):
    xq = mxq(f64(hidden_states), 2, "e4m3")
    q = (xq @ unpack4(Wq_words, Wq_scales)).reshape(B, S, H, HD)
    k = (xq @ unpack4(Wk_words, Wk_scales)).reshape(B, S, HKV, HD)
    v = (xq @ unpack4(Wv_words, Wv_scales)).reshape(B, S, HKV, HD)
    q = rms_norm(q, f64(q_scale))
    k = rms_norm(k, f64(k_scale))
    q = apply_rope(q, f64(cos), f64(sin))
    k = apply_rope(k, f64(cos), f64(sin))
    return q, k, v

@@ -1,0 +1,254 @@
+from contextlib import ExitStack
+
+import concourse.mybir as mybir
+from concourse.masks import make_identity
+
+F32 = mybir.dt.float32
+BF16 = mybir.dt.bfloat16
+I32 = mybir.dt.int32
+U32 = mybir.dt.uint32
+U8 = mybir.dt.uint8
+FP8X4 = mybir.dt.float8_e4m3fn_x4
+FP4X4 = mybir.dt.float4_e2m1fn_x4
+ALU = mybir.AluOpType
+ACT = mybir.ActivationFunctionType
+
+P = 128
+TOKENS = 512
+TOKEN_TILES = TOKENS // P
+D_MODEL = 2048
+PACK = 4
+K_PASS = P * PACK
+PASSES = D_MODEL // K_PASS
+HEAD = 128
+HALF = HEAD // 2
+BANK = 512
+BANK_HEADS = BANK // HEAD
+SLAB_BANKS = 2
+SLAB = SLAB_BANKS * BANK
+SLAB_HEADS = SLAB // HEAD
+EPS = 1e-6
+
+FLOPS = 2 * TOKENS * D_MODEL * (2048 + 1024 + 1024)
+
+
+def tile_multiheadattention_pa_kernel(
+    tc,
+    hidden_states,
+    cos,
+    sin,
+    Wq_words,
+    Wq_scales,
+    Wk_words,
+    Wk_scales,
+    Wv_words,
+    Wv_scales,
+    q_scale,
+    k_scale,
+    out_0,
+    out_1,
+    out_2,
+):
+    nc = tc.nc
+
+    x_dram = hidden_states[0].rearrange("(p m) d -> p m d", m=TOKEN_TILES)
+    cos_dram = cos[0].rearrange("(p m) j -> p m j", m=TOKEN_TILES)
+    sin_dram = sin[0].rearrange("(p m) j -> p m j", m=TOKEN_TILES)
+    q_dram = out_0[0].rearrange("(p m) h j -> p m (h j)", m=TOKEN_TILES)
+    k_dram = out_1[0].rearrange("(p m) h j -> p m (h j)", m=TOKEN_TILES)
+    v_dram = out_2[0].rearrange("(p m) h j -> p m (h j)", m=TOKEN_TILES)
+
+    slabs = (
+        {"words": Wq_words, "scales": Wq_scales, "first": 0, "out": q_dram, "gain": 0},
+        {"words": Wq_words, "scales": Wq_scales, "first": SLAB, "out": q_dram, "gain": 0},
+        {"words": Wk_words, "scales": Wk_scales, "first": 0, "out": k_dram, "gain": 1},
+        {"words": Wv_words, "scales": Wv_scales, "first": 0, "out": v_dram, "gain": None},
+    )
+
+    with ExitStack() as ctx:
+        ctx.enter_context(tc.manual_schedule())
+        resident = ctx.enter_context(tc.tile_pool(name="resident", bufs=1))
+        prep = ctx.enter_context(tc.tile_pool(name="prep", bufs=2))
+        small = ctx.enter_context(tc.tile_pool(name="small", bufs=4))
+        squares = ctx.enter_context(tc.tile_pool(name="squares", bufs=2))
+        products = ctx.enter_context(tc.tile_pool(name="products", bufs=6))
+        results = ctx.enter_context(tc.tile_pool(name="results", bufs=4))
+        psum = ctx.enter_context(tc.psum_pool(name="psum", bufs=8))
+
+        gain_rows = resident.tile([P, 2 * HEAD], BF16, name="gain_rows")
+        nc.vector.memset(gain_rows[:], 0.0)
+        ones = resident.tile([P, P], BF16, name="ones")
+        nc.vector.memset(ones[:], 1.0)
+        eps = resident.tile([P, 1], F32, name="eps")
+        nc.vector.memset(eps[:], EPS)
+        ident = resident.tile([P, P], F32, name="ident")
+        make_identity(nc, ident[:])
+
+        nc.scalar.dma_start(out=gain_rows[0:1, 0:HEAD], in_=q_scale.unsqueeze(0))
+        nc.scalar.dma_start(out=gain_rows[0:1, HEAD : 2 * HEAD], in_=k_scale.unsqueeze(0))
+        cos_sb = resident.tile([P, TOKEN_TILES, HEAD], BF16, name="cos_sb")
+        nc.scalar.dma_start(out=cos_sb[:], in_=cos_dram)
+        sin_sb = resident.tile([P, TOKEN_TILES, HEAD], BF16, name="sin_sb")
+        nc.scalar.dma_start(out=sin_sb[:], in_=sin_dram)
+
+        x_sb = []
+        for m in range(TOKEN_TILES):
+            x_tile = resident.tile([P, D_MODEL], BF16, name="x%d" % m)
+            nc.sync.dma_start(out=x_tile[:], in_=x_dram[:, m, :])
+            x_sb.append(x_tile)
+
+        w_words = []
+        w_planes = []
+        for s, slab in enumerate(slabs):
+            plane = resident.tile([P, PASSES, SLAB], U8, align_bytes=64, name="plane%d" % s)
+            nc.vector.memset(plane[:].bitcast(I32), 0)
+            rows = slab["scales"].bitcast(I32).rearrange("g (j q) n -> q j g n", q=8)
+            first_word = slab["first"] // 4
+            for q in range(8):
+                start = 32 * (q // 4) + q % 4
+                nc.sync.dma_start(
+                    out=plane[start:P:64, :, :].bitcast(I32),
+                    in_=rows[q, :, :, first_word : first_word + SLAB // 4],
+                )
+            w_planes.append(plane)
+
+            words = resident.tile([P, PASSES, 2 * SLAB], U8, align_bytes=64, name="words%d" % s)
+            source = slab["words"].bitcast(I32).rearrange("g p w -> p g w")
+            first_word = slab["first"] // 2
+            nc.sync.dma_start(
+                out=words[:].bitcast(I32), in_=source[:, :, first_word : first_word + SLAB // 2]
+            )
+            w_words.append(words)
+
+        warm = resident.tile([P, 1], F32, name="warm")
+        nc.scalar.activation(out=warm[:], in_=eps[:], func=ACT.Abs_reciprocal_sqrt)
+
+        gain_ps = psum.tile([P, BANK], F32, tag="bank", name="gain_ps")
+        nc.tensor.matmul(
+            out=gain_ps[:, 0 : 2 * HEAD], lhsT=ones[:], rhs=gain_rows[:], start=True, stop=True
+        )
+        gain_sb = resident.tile([P, 2 * HEAD], F32, name="gain_sb")
+        nc.scalar.copy(out=gain_sb[:], in_=gain_ps[:, 0 : 2 * HEAD])
+
+        x_codes = []
+        x_scales = []
+        for m in range(TOKEN_TILES):
+            x_pairs = x_sb[m][:].bitcast(F32)
+            grouped = prep.tile([P, PASSES, P, PACK], BF16, align_bytes=64, name="grouped")
+            grouped_pairs = grouped[:].bitcast(F32)
+            for b in range(2):
+                xt = psum.tile([P, 2, 2, P], F32, tag="bank", name="xt")
+                for i in range(2):
+                    g = 2 * b + i
+                    for u in range(2):
+                        nc.tensor.transpose(
+                            out=xt[:, i, u, :],
+                            in_=x_pairs[:, 256 * g + u : 256 * (g + 1) : 2],
+                            identity=ident[:],
+                        )
+                copy_out = nc.vector.tensor_copy if b == 0 else nc.scalar.copy
+                copy_out(
+                    out=grouped_pairs[:, 2 * b : 2 * b + 2, :, :],
+                    in_=xt[:].rearrange("p i u r -> p i r u"),
+                )
+            codes = resident.tile([P, PASSES, P], U32, align_bytes=64, name="x_codes%d" % m)
+            scales = resident.tile([P, PASSES, P], U8, align_bytes=64, name="x_scales%d" % m)
+            nc.vector.quantize_mx(
+                out=codes[:].rearrange("p g r -> p (g r)").bitcast(FP8X4),
+                scales=scales[:].rearrange("p g r -> p (g r)"),
+                in_=grouped[:].rearrange("p g r t -> p (g r t)"),
+            )
+            x_codes.append(codes)
+            x_scales.append(scales)
+
+        tables = []
+        for w in range(2):
+            gain = gain_sb[:, w * HEAD : (w + 1) * HEAD]
+            table = resident.tile([P, TOKEN_TILES, 2, HEAD], F32, name="table%d" % w)
+            nc.vector.tensor_tensor(
+                out=table[:, :, 0, :],
+                in0=cos_sb[:],
+                in1=gain.unsqueeze(1).to_broadcast([P, TOKEN_TILES, HEAD]),
+                op=ALU.mult,
+            )
+            nc.vector.tensor_tensor(
+                out=table[:, :, 1, 0:HALF],
+                in0=sin_sb[:, :, HALF:HEAD],
+                in1=gain[:, 0:HALF].unsqueeze(1).to_broadcast([P, TOKEN_TILES, HALF]),
+                op=ALU.mult,
+            )
+            nc.vector.scalar_tensor_tensor(
+                out=table[:, :, 1, HALF:HEAD],
+                in0=sin_sb[:, :, 0:HALF],
+                scalar=-1.0,
+                in1=gain[:, HALF:HEAD].unsqueeze(1).to_broadcast([P, TOKEN_TILES, HALF]),
+                op0=ALU.mult,
+                op1=ALU.mult,
+            )
+            tables.append(table)
+
+        for s, slab in enumerate(slabs):
+            for m in range(TOKEN_TILES):
+                banks = []
+                for b in range(SLAB_BANKS):
+                    acc = psum.tile([P, BANK], F32, tag="bank", name="acc")
+                    for g in range(PASSES):
+                        nc.tensor.matmul_mx(
+                            out=acc[:],
+                            lhsT=x_codes[m][:, g, :].bitcast(FP8X4),
+                            lhsT_scale=x_scales[m][:, g, :],
+                            rhs=w_words[s][:, g, 2 * BANK * b : 2 * BANK * (b + 1)].bitcast(FP4X4),
+                            rhs_scale=w_planes[s][:, g, BANK * b : BANK * (b + 1)],
+                            start=(g == 0),
+                            stop=(g == PASSES - 1),
+                        )
+                    banks.append(acc)
+
+                result = results.tile([P, SLAB_HEADS, HEAD], F32, name="result")
+                if slab["gain"] is None:
+                    flat = result[:].rearrange("p h j -> p (h j)")
+                    nc.scalar.copy(out=flat[:, 0:BANK], in_=banks[0][:])
+                    nc.vector.tensor_copy(out=flat[:, BANK:SLAB], in_=banks[1][:])
+                else:
+                    squared = squares.tile([P, SLAB_HEADS, HEAD], F32, name="squared")
+                    sums = small.tile([P, SLAB_HEADS], F32, name="sums")
+                    for h in range(SLAB_HEADS):
+                        head = banks[h // BANK_HEADS][:, (h % BANK_HEADS) * HEAD : (h % BANK_HEADS + 1) * HEAD]
+                        nc.scalar.activation(
+                            out=squared[:, h, :], in_=head, func=ACT.Square, accum_out=sums[:, h : h + 1]
+                        )
+                    inv_rms = small.tile([P, SLAB_HEADS], F32, name="inv_rms")
+                    nc.scalar.activation(
+                        out=inv_rms[:],
+                        in_=sums[:],
+                        func=ACT.Abs_reciprocal_sqrt,
+                        scale=1.0 / HEAD,
+                        bias=eps[:],
+                    )
+                    shares = products.tile([P, SLAB_HEADS, 2, HEAD], F32, name="shares")
+                    for h in range(SLAB_HEADS):
+                        head = banks[h // BANK_HEADS][:, (h % BANK_HEADS) * HEAD : (h % BANK_HEADS + 1) * HEAD]
+                        nc.vector.scalar_tensor_tensor(
+                            out=shares[:, h, :, :],
+                            in0=head.unsqueeze(1).to_broadcast([P, 2, HEAD]),
+                            scalar=inv_rms[:, h : h + 1],
+                            in1=tables[slab["gain"]][:, m, :, :],
+                            op0=ALU.mult,
+                            op1=ALU.mult,
+                        )
+                    nc.gpsimd.tensor_tensor(
+                        out=result[:, :, 0:HALF],
+                        in0=shares[:, :, 0, 0:HALF],
+                        in1=shares[:, :, 1, HALF:HEAD],
+                        op=ALU.add,
+                    )
+                    nc.gpsimd.tensor_tensor(
+                        out=result[:, :, HALF:HEAD],
+                        in0=shares[:, :, 0, HALF:HEAD],
+                        in1=shares[:, :, 1, 0:HALF],
+                        op=ALU.add,
+                    )
+                nc.sync.dma_start(
+                    out=slab["out"][:, m, slab["first"] : slab["first"] + SLAB],
+                    in_=result[:].rearrange("p h j -> p (h j)"),
+                )

@@ -28,6 +28,7 @@ SLAB_BANKS = 2
 SLAB = SLAB_BANKS * BANK
 SLAB_HEADS = SLAB // HEAD
 EPS = 1e-6
+LAST_NORMED_SLAB = 2
 
 FLOPS = 2 * TOKENS * D_MODEL * (2048 + 1024 + 1024)
 
@@ -73,6 +74,7 @@ def tile_multiheadattention_pa_kernel(
         squares = ctx.enter_context(tc.tile_pool(name="squares", bufs=2))
         products = ctx.enter_context(tc.tile_pool(name="products", bufs=6))
         results = ctx.enter_context(tc.tile_pool(name="results", bufs=4))
+        copies = ctx.enter_context(tc.tile_pool(name="copies", bufs=4))
         psum = ctx.enter_context(tc.psum_pool(name="psum", bufs=8))
 
         gain_rows = resident.tile([P, 2 * HEAD], BF16, name="gain_rows")
@@ -86,10 +88,6 @@ def tile_multiheadattention_pa_kernel(
 
         nc.scalar.dma_start(out=gain_rows[0:1, 0:HEAD], in_=q_scale.unsqueeze(0))
         nc.scalar.dma_start(out=gain_rows[0:1, HEAD : 2 * HEAD], in_=k_scale.unsqueeze(0))
-        cos_sb = resident.tile([P, TOKEN_TILES, HEAD], BF16, name="cos_sb")
-        nc.scalar.dma_start(out=cos_sb[:], in_=cos_dram)
-        sin_sb = resident.tile([P, TOKEN_TILES, HEAD], BF16, name="sin_sb")
-        nc.scalar.dma_start(out=sin_sb[:], in_=sin_dram)
 
         x_sb = []
         for m in range(TOKEN_TILES):
@@ -97,38 +95,39 @@ def tile_multiheadattention_pa_kernel(
             nc.sync.dma_start(out=x_tile[:], in_=x_dram[:, m, :])
             x_sb.append(x_tile)
 
+        cos_sb = resident.tile([P, TOKEN_TILES, HEAD], BF16, name="cos_sb")
+        sin_sb = resident.tile([P, TOKEN_TILES, HEAD], BF16, name="sin_sb")
         w_words = []
         w_planes = []
         for s, slab in enumerate(slabs):
             plane = resident.tile([P, PASSES, SLAB], U8, align_bytes=64, name="plane%d" % s)
             nc.vector.memset(plane[:].bitcast(I32), 0)
-            rows = slab["scales"].bitcast(I32).rearrange("g (j q) n -> q j g n", q=8)
+            rows = slab["scales"].bitcast(I32).rearrange("g (c r) n -> r c g n", r=4)
             first_word = slab["first"] // 4
-            for q in range(8):
-                start = 32 * (q // 4) + q % 4
+            for r in range(4):
                 nc.sync.dma_start(
-                    out=plane[start:P:64, :, :].bitcast(I32),
-                    in_=rows[q, :, :, first_word : first_word + SLAB // 4],
+                    out=plane[r:P:32, :, :].bitcast(I32),
+                    in_=rows[r, :, :, first_word : first_word + SLAB // 4],
                 )
             w_planes.append(plane)
 
-            words = resident.tile([P, PASSES, 2 * SLAB], U8, align_bytes=64, name="words%d" % s)
             source = slab["words"].bitcast(I32).rearrange("g p w -> p g w")
-            first_word = slab["first"] // 2
-            nc.sync.dma_start(
-                out=words[:].bitcast(I32), in_=source[:, :, first_word : first_word + SLAB // 2]
-            )
-            w_words.append(words)
+            bank_words = []
+            for b in range(SLAB_BANKS):
+                words = resident.tile([P, PASSES, 2 * BANK], U8, align_bytes=64, name="words%d_%d" % (s, b))
+                first_word = (slab["first"] + b * BANK) // 2
+                nc.sync.dma_start(
+                    out=words[:].bitcast(I32), in_=source[:, :, first_word : first_word + BANK // 2]
+                )
+                bank_words.append(words)
+            w_words.append(bank_words)
+
+            if s == 0:
+                nc.sync.dma_start(out=cos_sb[:], in_=cos_dram)
+                nc.sync.dma_start(out=sin_sb[:], in_=sin_dram)
 
         warm = resident.tile([P, 1], F32, name="warm")
         nc.scalar.activation(out=warm[:], in_=eps[:], func=ACT.Abs_reciprocal_sqrt)
-
-        gain_ps = psum.tile([P, BANK], F32, tag="bank", name="gain_ps")
-        nc.tensor.matmul(
-            out=gain_ps[:, 0 : 2 * HEAD], lhsT=ones[:], rhs=gain_rows[:], start=True, stop=True
-        )
-        gain_sb = resident.tile([P, 2 * HEAD], F32, name="gain_sb")
-        nc.scalar.copy(out=gain_sb[:], in_=gain_ps[:, 0 : 2 * HEAD])
 
         x_codes = []
         x_scales = []
@@ -160,6 +159,13 @@ def tile_multiheadattention_pa_kernel(
             )
             x_codes.append(codes)
             x_scales.append(scales)
+
+        gain_ps = psum.tile([P, BANK], F32, tag="bank", name="gain_ps")
+        nc.tensor.matmul(
+            out=gain_ps[:, 0 : 2 * HEAD], lhsT=ones[:], rhs=gain_rows[:], start=True, stop=True
+        )
+        gain_sb = resident.tile([P, 2 * HEAD], F32, name="gain_sb")
+        nc.scalar.copy(out=gain_sb[:], in_=gain_ps[:, 0 : 2 * HEAD])
 
         tables = []
         for w in range(2):
@@ -197,18 +203,20 @@ def tile_multiheadattention_pa_kernel(
                             out=acc[:],
                             lhsT=x_codes[m][:, g, :].bitcast(FP8X4),
                             lhsT_scale=x_scales[m][:, g, :],
-                            rhs=w_words[s][:, g, 2 * BANK * b : 2 * BANK * (b + 1)].bitcast(FP4X4),
+                            rhs=w_words[s][b][:, g, :].bitcast(FP4X4),
                             rhs_scale=w_planes[s][:, g, BANK * b : BANK * (b + 1)],
                             start=(g == 0),
                             stop=(g == PASSES - 1),
                         )
                     banks.append(acc)
 
-                result = results.tile([P, SLAB_HEADS, HEAD], F32, name="result")
                 if slab["gain"] is None:
-                    flat = result[:].rearrange("p h j -> p (h j)")
-                    nc.scalar.copy(out=flat[:, 0:BANK], in_=banks[0][:])
-                    nc.vector.tensor_copy(out=flat[:, BANK:SLAB], in_=banks[1][:])
+                    for b in range(SLAB_BANKS):
+                        copied = copies.tile([P, BANK], F32, name="copied")
+                        nc.scalar.copy(out=copied[:], in_=banks[b][:])
+                        nc.sync.dma_start(
+                            out=slab["out"][:, m, b * BANK : (b + 1) * BANK], in_=copied[:]
+                        )
                 else:
                     squared = squares.tile([P, SLAB_HEADS, HEAD], F32, name="squared")
                     sums = small.tile([P, SLAB_HEADS], F32, name="sums")
@@ -236,19 +244,21 @@ def tile_multiheadattention_pa_kernel(
                             op0=ALU.mult,
                             op1=ALU.mult,
                         )
+                    result = results.tile([P, SLAB_HEADS, HEAD], F32, name="result")
+                    upper_adder = nc.vector if s == LAST_NORMED_SLAB else nc.gpsimd
                     nc.gpsimd.tensor_tensor(
                         out=result[:, :, 0:HALF],
                         in0=shares[:, :, 0, 0:HALF],
                         in1=shares[:, :, 1, HALF:HEAD],
                         op=ALU.add,
                     )
-                    nc.gpsimd.tensor_tensor(
+                    upper_adder.tensor_tensor(
                         out=result[:, :, HALF:HEAD],
                         in0=shares[:, :, 0, HALF:HEAD],
                         in1=shares[:, :, 1, 0:HALF],
                         op=ALU.add,
                     )
-                nc.sync.dma_start(
-                    out=slab["out"][:, m, slab["first"] : slab["first"] + SLAB],
-                    in_=result[:].rearrange("p h j -> p (h j)"),
-                )
+                    nc.sync.dma_start(
+                        out=slab["out"][:, m, slab["first"] : slab["first"] + SLAB],
+                        in_=result[:].rearrange("p h j -> p (h j)"),
+                    )

@@ -74,7 +74,7 @@ def tile_multiheadattention_pa_kernel(
         squares = ctx.enter_context(tc.tile_pool(name="squares", bufs=2))
         products = ctx.enter_context(tc.tile_pool(name="products", bufs=6))
         results = ctx.enter_context(tc.tile_pool(name="results", bufs=4))
-        copies = ctx.enter_context(tc.tile_pool(name="copies", bufs=4))
+        copies = ctx.enter_context(tc.tile_pool(name="copies", bufs=8))
         psum = ctx.enter_context(tc.psum_pool(name="psum", bufs=8))
 
         gain_rows = resident.tile([P, 2 * HEAD], BF16, name="gain_rows")
@@ -102,12 +102,13 @@ def tile_multiheadattention_pa_kernel(
         for s, slab in enumerate(slabs):
             plane = resident.tile([P, PASSES, SLAB], U8, align_bytes=64, name="plane%d" % s)
             nc.vector.memset(plane[:].bitcast(I32), 0)
-            rows = slab["scales"].bitcast(I32).rearrange("g (c r) n -> r c g n", r=4)
+            rows = slab["scales"].bitcast(I32).rearrange("g (j q) n -> q j g n", q=8)
             first_word = slab["first"] // 4
-            for r in range(4):
+            for q in range(8):
+                start = 32 * (q // 4) + q % 4
                 nc.sync.dma_start(
-                    out=plane[r:P:32, :, :].bitcast(I32),
-                    in_=rows[r, :, :, first_word : first_word + SLAB // 4],
+                    out=plane[start:P:64, :, :].bitcast(I32),
+                    in_=rows[q, :, :, first_word : first_word + SLAB // 4],
                 )
             w_planes.append(plane)
 
@@ -214,7 +215,7 @@ def tile_multiheadattention_pa_kernel(
                     for b in range(SLAB_BANKS):
                         copied = copies.tile([P, BANK], F32, name="copied")
                         nc.scalar.copy(out=copied[:], in_=banks[b][:])
-                        nc.sync.dma_start(
+                        nc.scalar.dma_start(
                             out=slab["out"][:, m, b * BANK : (b + 1) * BANK], in_=copied[:]
                         )
                 else:

@@ -92,7 +92,8 @@ def tile_multiheadattention_pa_kernel(
         x_sb = []
         for m in range(TOKEN_TILES):
             x_tile = resident.tile([P, D_MODEL], BF16, name="x%d" % m)
-            nc.sync.dma_start(out=x_tile[:], in_=x_dram[:, m, :])
+            x_queue = nc.scalar if m < TOKEN_TILES // 2 else nc.gpsimd
+            x_queue.dma_start(out=x_tile[:], in_=x_dram[:, m, :])
             x_sb.append(x_tile)
 
         cos_sb = resident.tile([P, TOKEN_TILES, HEAD], BF16, name="cos_sb")

@@ -28,7 +28,8 @@ SLAB_BANKS = 2
 SLAB = SLAB_BANKS * BANK
 SLAB_HEADS = SLAB // HEAD
 EPS = 1e-6
-LAST_NORMED_SLAB = 2
+NORMED_SLABS = 3
+HELPED_UNITS = 2
 
 FLOPS = 2 * TOKENS * D_MODEL * (2048 + 1024 + 1024)
 
@@ -70,37 +71,18 @@ def tile_multiheadattention_pa_kernel(
         ctx.enter_context(tc.manual_schedule())
         resident = ctx.enter_context(tc.tile_pool(name="resident", bufs=1))
         prep = ctx.enter_context(tc.tile_pool(name="prep", bufs=2))
-        small = ctx.enter_context(tc.tile_pool(name="small", bufs=4))
-        squares = ctx.enter_context(tc.tile_pool(name="squares", bufs=2))
+        small = ctx.enter_context(tc.tile_pool(name="small", bufs=6))
+        squares = ctx.enter_context(tc.tile_pool(name="squares", bufs=3))
         products = ctx.enter_context(tc.tile_pool(name="products", bufs=6))
         results = ctx.enter_context(tc.tile_pool(name="results", bufs=4))
         copies = ctx.enter_context(tc.tile_pool(name="copies", bufs=8))
         psum = ctx.enter_context(tc.psum_pool(name="psum", bufs=8))
 
-        gain_rows = resident.tile([P, 2 * HEAD], BF16, name="gain_rows")
-        nc.vector.memset(gain_rows[:], 0.0)
-        ones = resident.tile([P, P], BF16, name="ones")
-        nc.vector.memset(ones[:], 1.0)
-        eps = resident.tile([P, 1], F32, name="eps")
-        nc.vector.memset(eps[:], EPS)
-        ident = resident.tile([P, P], F32, name="ident")
-        make_identity(nc, ident[:])
-
-        nc.scalar.dma_start(out=gain_rows[0:1, 0:HEAD], in_=q_scale.unsqueeze(0))
-        nc.scalar.dma_start(out=gain_rows[0:1, HEAD : 2 * HEAD], in_=k_scale.unsqueeze(0))
-
-        x_sb = []
-        for m in range(TOKEN_TILES):
-            x_tile = resident.tile([P, D_MODEL], BF16, name="x%d" % m)
-            x_queue = nc.scalar if m < TOKEN_TILES // 2 else nc.gpsimd
-            x_queue.dma_start(out=x_tile[:], in_=x_dram[:, m, :])
-            x_sb.append(x_tile)
-
-        cos_sb = resident.tile([P, TOKEN_TILES, HEAD], BF16, name="cos_sb")
-        sin_sb = resident.tile([P, TOKEN_TILES, HEAD], BF16, name="sin_sb")
         w_words = []
         w_planes = []
-        for s, slab in enumerate(slabs):
+
+        def load_slab(s):
+            slab = slabs[s]
             plane = resident.tile([P, PASSES, SLAB], U8, align_bytes=64, name="plane%d" % s)
             nc.vector.memset(plane[:].bitcast(I32), 0)
             rows = slab["scales"].bitcast(I32).rearrange("g (j q) n -> q j g n", q=8)
@@ -124,43 +106,31 @@ def tile_multiheadattention_pa_kernel(
                 bank_words.append(words)
             w_words.append(bank_words)
 
-            if s == 0:
-                nc.sync.dma_start(out=cos_sb[:], in_=cos_dram)
-                nc.sync.dma_start(out=sin_sb[:], in_=sin_dram)
+        gain_rows = resident.tile([P, 2 * HEAD], BF16, name="gain_rows")
+        nc.vector.memset(gain_rows[:], 0.0)
+        ones = resident.tile([P, P], BF16, name="ones")
+        nc.vector.memset(ones[:], 1.0)
+        eps = resident.tile([P, 1], F32, name="eps")
+        nc.vector.memset(eps[:], EPS)
+        ident = resident.tile([P, P], F32, name="ident")
+        make_identity(nc, ident[:])
+
+        nc.scalar.dma_start(out=gain_rows[0:1, 0:HEAD], in_=q_scale.unsqueeze(0))
+        nc.scalar.dma_start(out=gain_rows[0:1, HEAD : 2 * HEAD], in_=k_scale.unsqueeze(0))
+        cos_sb = resident.tile([P, TOKEN_TILES, HEAD], BF16, name="cos_sb")
+        nc.scalar.dma_start(out=cos_sb[:], in_=cos_dram)
+        sin_sb = resident.tile([P, TOKEN_TILES, HEAD], BF16, name="sin_sb")
+        nc.scalar.dma_start(out=sin_sb[:], in_=sin_dram)
+        x_sb = []
+        for m in range(TOKEN_TILES):
+            x_tile = resident.tile([P, D_MODEL], BF16, name="x%d" % m)
+            x_queue = nc.scalar if m < TOKEN_TILES // 2 else nc.gpsimd
+            x_queue.dma_start(out=x_tile[:], in_=x_dram[:, m, :])
+            x_sb.append(x_tile)
+        load_slab(0)
 
         warm = resident.tile([P, 1], F32, name="warm")
         nc.scalar.activation(out=warm[:], in_=eps[:], func=ACT.Abs_reciprocal_sqrt)
-
-        x_codes = []
-        x_scales = []
-        for m in range(TOKEN_TILES):
-            x_pairs = x_sb[m][:].bitcast(F32)
-            grouped = prep.tile([P, PASSES, P, PACK], BF16, align_bytes=64, name="grouped")
-            grouped_pairs = grouped[:].bitcast(F32)
-            for b in range(2):
-                xt = psum.tile([P, 2, 2, P], F32, tag="bank", name="xt")
-                for i in range(2):
-                    g = 2 * b + i
-                    for u in range(2):
-                        nc.tensor.transpose(
-                            out=xt[:, i, u, :],
-                            in_=x_pairs[:, 256 * g + u : 256 * (g + 1) : 2],
-                            identity=ident[:],
-                        )
-                copy_out = nc.vector.tensor_copy if b == 0 else nc.scalar.copy
-                copy_out(
-                    out=grouped_pairs[:, 2 * b : 2 * b + 2, :, :],
-                    in_=xt[:].rearrange("p i u r -> p i r u"),
-                )
-            codes = resident.tile([P, PASSES, P], U32, align_bytes=64, name="x_codes%d" % m)
-            scales = resident.tile([P, PASSES, P], U8, align_bytes=64, name="x_scales%d" % m)
-            nc.vector.quantize_mx(
-                out=codes[:].rearrange("p g r -> p (g r)").bitcast(FP8X4),
-                scales=scales[:].rearrange("p g r -> p (g r)"),
-                in_=grouped[:].rearrange("p g r t -> p (g r t)"),
-            )
-            x_codes.append(codes)
-            x_scales.append(scales)
 
         gain_ps = psum.tile([P, BANK], F32, tag="bank", name="gain_ps")
         nc.tensor.matmul(
@@ -195,6 +165,39 @@ def tile_multiheadattention_pa_kernel(
             )
             tables.append(table)
 
+        for s in range(1, len(slabs)):
+            load_slab(s)
+
+        x_codes = []
+        x_scales = []
+        for m in range(TOKEN_TILES):
+            x_pairs = x_sb[m][:].bitcast(F32)
+            grouped = prep.tile([P, PASSES, P, PACK], BF16, align_bytes=64, name="grouped")
+            grouped_pairs = grouped[:].bitcast(F32)
+            for b in range(2):
+                xt = psum.tile([P, 2, 2, P], F32, tag="bank", name="xt")
+                for i in range(2):
+                    g = 2 * b + i
+                    for u in range(2):
+                        nc.tensor.transpose(
+                            out=xt[:, i, u, :],
+                            in_=x_pairs[:, 256 * g + u : 256 * (g + 1) : 2],
+                            identity=ident[:],
+                        )
+                nc.scalar.copy(
+                    out=grouped_pairs[:, 2 * b : 2 * b + 2, :, :],
+                    in_=xt[:].rearrange("p i u r -> p i r u"),
+                )
+            codes = resident.tile([P, PASSES, P], U32, align_bytes=64, name="x_codes%d" % m)
+            scales = resident.tile([P, PASSES, P], U8, align_bytes=64, name="x_scales%d" % m)
+            nc.vector.quantize_mx(
+                out=codes[:].rearrange("p g r -> p (g r)").bitcast(FP8X4),
+                scales=scales[:].rearrange("p g r -> p (g r)"),
+                in_=grouped[:].rearrange("p g r t -> p (g r t)"),
+            )
+            x_codes.append(codes)
+            x_scales.append(scales)
+
         for s, slab in enumerate(slabs):
             for m in range(TOKEN_TILES):
                 banks = []
@@ -220,34 +223,37 @@ def tile_multiheadattention_pa_kernel(
                             out=slab["out"][:, m, b * BANK : (b + 1) * BANK], in_=copied[:]
                         )
                 else:
-                    squared = squares.tile([P, SLAB_HEADS, HEAD], F32, name="squared")
-                    sums = small.tile([P, SLAB_HEADS], F32, name="sums")
-                    for h in range(SLAB_HEADS):
-                        head = banks[h // BANK_HEADS][:, (h % BANK_HEADS) * HEAD : (h % BANK_HEADS + 1) * HEAD]
-                        nc.scalar.activation(
-                            out=squared[:, h, :], in_=head, func=ACT.Square, accum_out=sums[:, h : h + 1]
-                        )
-                    inv_rms = small.tile([P, SLAB_HEADS], F32, name="inv_rms")
-                    nc.scalar.activation(
-                        out=inv_rms[:],
-                        in_=sums[:],
-                        func=ACT.Abs_reciprocal_sqrt,
-                        scale=1.0 / HEAD,
-                        bias=eps[:],
-                    )
                     shares = products.tile([P, SLAB_HEADS, 2, HEAD], F32, name="shares")
-                    for h in range(SLAB_HEADS):
-                        head = banks[h // BANK_HEADS][:, (h % BANK_HEADS) * HEAD : (h % BANK_HEADS + 1) * HEAD]
-                        nc.vector.scalar_tensor_tensor(
-                            out=shares[:, h, :, :],
-                            in0=head.unsqueeze(1).to_broadcast([P, 2, HEAD]),
-                            scalar=inv_rms[:, h : h + 1],
-                            in1=tables[slab["gain"]][:, m, :, :],
-                            op0=ALU.mult,
-                            op1=ALU.mult,
+                    for b in range(SLAB_BANKS):
+                        squared = squares.tile([P, BANK_HEADS, HEAD], F32, name="squared")
+                        sums = small.tile([P, BANK_HEADS], F32, name="sums")
+                        for h in range(BANK_HEADS):
+                            nc.scalar.activation(
+                                out=squared[:, h, :],
+                                in_=banks[b][:, h * HEAD : (h + 1) * HEAD],
+                                func=ACT.Square,
+                                accum_out=sums[:, h : h + 1],
+                            )
+                        inv_rms = small.tile([P, BANK_HEADS], F32, name="inv_rms")
+                        nc.scalar.activation(
+                            out=inv_rms[:],
+                            in_=sums[:],
+                            func=ACT.Abs_reciprocal_sqrt,
+                            scale=1.0 / HEAD,
+                            bias=eps[:],
                         )
+                        for h in range(BANK_HEADS):
+                            nc.vector.scalar_tensor_tensor(
+                                out=shares[:, b * BANK_HEADS + h, :, :],
+                                in0=banks[b][:, h * HEAD : (h + 1) * HEAD].unsqueeze(1).to_broadcast([P, 2, HEAD]),
+                                scalar=inv_rms[:, h : h + 1],
+                                in1=tables[slab["gain"]][:, m, :, :],
+                                op0=ALU.mult,
+                                op1=ALU.mult,
+                            )
                     result = results.tile([P, SLAB_HEADS, HEAD], F32, name="result")
-                    upper_adder = nc.vector if s == LAST_NORMED_SLAB else nc.gpsimd
+                    units_left = (NORMED_SLABS - s) * TOKEN_TILES - m
+                    upper_adder = nc.vector if units_left <= HELPED_UNITS else nc.gpsimd
                     nc.gpsimd.tensor_tensor(
                         out=result[:, :, 0:HALF],
                         in0=shares[:, :, 0, 0:HALF],

@@ -29,7 +29,7 @@ SLAB = SLAB_BANKS * BANK
 SLAB_HEADS = SLAB // HEAD
 EPS = 1e-6
 NORMED_SLABS = 3
-HELPED_UNITS = 2
+HELPED_UNITS = 1
 
 FLOPS = 2 * TOKENS * D_MODEL * (2048 + 1024 + 1024)
 
@@ -74,7 +74,7 @@ def tile_multiheadattention_pa_kernel(
         small = ctx.enter_context(tc.tile_pool(name="small", bufs=6))
         squares = ctx.enter_context(tc.tile_pool(name="squares", bufs=3))
         products = ctx.enter_context(tc.tile_pool(name="products", bufs=6))
-        results = ctx.enter_context(tc.tile_pool(name="results", bufs=4))
+        results = ctx.enter_context(tc.tile_pool(name="results", bufs=6))
         copies = ctx.enter_context(tc.tile_pool(name="copies", bufs=8))
         psum = ctx.enter_context(tc.psum_pool(name="psum", bufs=8))
 
@@ -252,21 +252,22 @@ def tile_multiheadattention_pa_kernel(
                                 op1=ALU.mult,
                             )
                     result = results.tile([P, SLAB_HEADS, HEAD], F32, name="result")
+                    total = result[:].rearrange("p h (a j) -> p h a j", a=2)
+                    own = shares[:, :, 0, :].rearrange("p h (a j) -> p h a j", a=2)
+                    other = shares[:, :, 1, :].rearrange("p h (a j) -> p h a j", a=2)[:, :, ::-1, :]
                     units_left = (NORMED_SLABS - s) * TOKEN_TILES - m
-                    upper_adder = nc.vector if units_left <= HELPED_UNITS else nc.gpsimd
-                    nc.gpsimd.tensor_tensor(
-                        out=result[:, :, 0:HALF],
-                        in0=shares[:, :, 0, 0:HALF],
-                        in1=shares[:, :, 1, HALF:HEAD],
-                        op=ALU.add,
-                    )
-                    upper_adder.tensor_tensor(
-                        out=result[:, :, HALF:HEAD],
-                        in0=shares[:, :, 0, HALF:HEAD],
-                        in1=shares[:, :, 1, 0:HALF],
-                        op=ALU.add,
-                    )
-                    nc.sync.dma_start(
-                        out=slab["out"][:, m, slab["first"] : slab["first"] + SLAB],
-                        in_=result[:].rearrange("p h j -> p (h j)"),
-                    )
+                    if units_left <= HELPED_UNITS:
+                        nc.gpsimd.tensor_tensor(
+                            out=total[:, 0:BANK_HEADS], in0=own[:, 0:BANK_HEADS], in1=other[:, 0:BANK_HEADS], op=ALU.add
+                        )
+                        nc.vector.tensor_tensor(
+                            out=total[:, BANK_HEADS:], in0=own[:, BANK_HEADS:], in1=other[:, BANK_HEADS:], op=ALU.add
+                        )
+                    else:
+                        nc.gpsimd.tensor_tensor(out=total, in0=own, in1=other, op=ALU.add)
+                    for b in range(SLAB_BANKS):
+                        first = slab["first"] + b * BANK
+                        nc.sync.dma_start(
+                            out=slab["out"][:, m, first : first + BANK],
+                            in_=result[:, b * BANK_HEADS : (b + 1) * BANK_HEADS, :].rearrange("p h j -> p (h j)"),
+                        )

@@ -75,7 +75,7 @@ def tile_multiheadattention_pa_kernel(
         squares = ctx.enter_context(tc.tile_pool(name="squares", bufs=3))
         products = ctx.enter_context(tc.tile_pool(name="products", bufs=6))
         results = ctx.enter_context(tc.tile_pool(name="results", bufs=6))
-        copies = ctx.enter_context(tc.tile_pool(name="copies", bufs=8))
+        copies = ctx.enter_context(tc.tile_pool(name="copies", bufs=4))
         psum = ctx.enter_context(tc.psum_pool(name="psum", bufs=8))
 
         w_words = []
@@ -216,12 +216,10 @@ def tile_multiheadattention_pa_kernel(
                     banks.append(acc)
 
                 if slab["gain"] is None:
+                    copied = copies.tile([P, SLAB], F32, name="copied")
                     for b in range(SLAB_BANKS):
-                        copied = copies.tile([P, BANK], F32, name="copied")
-                        nc.scalar.copy(out=copied[:], in_=banks[b][:])
-                        nc.scalar.dma_start(
-                            out=slab["out"][:, m, b * BANK : (b + 1) * BANK], in_=copied[:]
-                        )
+                        nc.scalar.copy(out=copied[:, b * BANK : (b + 1) * BANK], in_=banks[b][:])
+                    nc.scalar.dma_start(out=slab["out"][:, m, :], in_=copied[:])
                 else:
                     shares = products.tile([P, SLAB_HEADS, 2, HEAD], F32, name="shares")
                     for b in range(SLAB_BANKS):
@@ -265,9 +263,7 @@ def tile_multiheadattention_pa_kernel(
                         )
                     else:
                         nc.gpsimd.tensor_tensor(out=total, in0=own, in1=other, op=ALU.add)
-                    for b in range(SLAB_BANKS):
-                        first = slab["first"] + b * BANK
-                        nc.sync.dma_start(
-                            out=slab["out"][:, m, first : first + BANK],
-                            in_=result[:, b * BANK_HEADS : (b + 1) * BANK_HEADS, :].rearrange("p h j -> p (h j)"),
-                        )
+                    nc.sync.dma_start(
+                        out=slab["out"][:, m, slab["first"] : slab["first"] + SLAB],
+                        in_=result[:].rearrange("p h j -> p (h j)"),
+                    )

@@ -70,7 +70,7 @@ def tile_multiheadattention_pa_kernel(
     with ExitStack() as ctx:
         ctx.enter_context(tc.manual_schedule())
         resident = ctx.enter_context(tc.tile_pool(name="resident", bufs=1))
-        prep = ctx.enter_context(tc.tile_pool(name="prep", bufs=2))
+        prep = ctx.enter_context(tc.tile_pool(name="prep", bufs=4))
         small = ctx.enter_context(tc.tile_pool(name="small", bufs=6))
         squares = ctx.enter_context(tc.tile_pool(name="squares", bufs=3))
         products = ctx.enter_context(tc.tile_pool(name="products", bufs=6))
@@ -81,19 +81,21 @@ def tile_multiheadattention_pa_kernel(
         w_words = []
         w_planes = []
 
-        def load_slab(s):
-            slab = slabs[s]
+        def zero_plane(s):
             plane = resident.tile([P, PASSES, SLAB], U8, align_bytes=64, name="plane%d" % s)
             nc.vector.memset(plane[:].bitcast(I32), 0)
-            rows = slab["scales"].bitcast(I32).rearrange("g (j q) n -> q j g n", q=8)
-            first_word = slab["first"] // 4
-            for q in range(8):
-                start = 32 * (q // 4) + q % 4
-                nc.sync.dma_start(
-                    out=plane[start:P:64, :, :].bitcast(I32),
-                    in_=rows[q, :, :, first_word : first_word + SLAB // 4],
-                )
             w_planes.append(plane)
+
+        def load_slab(s):
+            slab = slabs[s]
+            plane = w_planes[s]
+            rows = slab["scales"].bitcast(I32).rearrange("g (j r) n -> r j g n", r=4)
+            first_word = slab["first"] // 4
+            for r in range(4):
+                nc.sync.dma_start(
+                    out=plane[r:P:32, :, :].bitcast(I32),
+                    in_=rows[r, :, :, first_word : first_word + SLAB // 4],
+                )
 
             source = slab["words"].bitcast(I32).rearrange("g p w -> p g w")
             bank_words = []
@@ -115,32 +117,43 @@ def tile_multiheadattention_pa_kernel(
         ident = resident.tile([P, P], F32, name="ident")
         make_identity(nc, ident[:])
 
-        nc.scalar.dma_start(out=gain_rows[0:1, 0:HEAD], in_=q_scale.unsqueeze(0))
-        nc.scalar.dma_start(out=gain_rows[0:1, HEAD : 2 * HEAD], in_=k_scale.unsqueeze(0))
-        cos_sb = resident.tile([P, TOKEN_TILES, HEAD], BF16, name="cos_sb")
-        nc.scalar.dma_start(out=cos_sb[:], in_=cos_dram)
-        sin_sb = resident.tile([P, TOKEN_TILES, HEAD], BF16, name="sin_sb")
-        nc.scalar.dma_start(out=sin_sb[:], in_=sin_dram)
+        for s in range(len(slabs)):
+            zero_plane(s)
+
         x_sb = []
         for m in range(TOKEN_TILES):
             x_tile = resident.tile([P, D_MODEL], BF16, name="x%d" % m)
-            x_queue = nc.scalar if m < TOKEN_TILES // 2 else nc.gpsimd
-            x_queue.dma_start(out=x_tile[:], in_=x_dram[:, m, :])
             x_sb.append(x_tile)
+        for half in range(2):
+            columns = slice(half * D_MODEL // 2, (half + 1) * D_MODEL // 2)
+            nc.sync.dma_start(out=x_sb[0][:, columns], in_=x_dram[:, 0, columns])
+        nc.sync.dma_start(out=gain_rows[0:1, 0:HEAD], in_=q_scale.unsqueeze(0))
+        nc.sync.dma_start(out=gain_rows[0:1, HEAD : 2 * HEAD], in_=k_scale.unsqueeze(0))
+        for m in range(1, TOKEN_TILES):
+            nc.sync.dma_start(out=x_sb[m][:], in_=x_dram[:, m, :])
         load_slab(0)
+        cos_sb = resident.tile([P, TOKEN_TILES, HEAD], BF16, name="cos_sb")
+        nc.sync.dma_start(out=cos_sb[:], in_=cos_dram)
+        sin_sb = resident.tile([P, TOKEN_TILES, HEAD], BF16, name="sin_sb")
+        nc.sync.dma_start(out=sin_sb[:], in_=sin_dram)
+        for s in range(1, len(slabs)):
+            load_slab(s)
 
         warm = resident.tile([P, 1], F32, name="warm")
         nc.scalar.activation(out=warm[:], in_=eps[:], func=ACT.Abs_reciprocal_sqrt)
 
-        gain_ps = psum.tile([P, BANK], F32, tag="bank", name="gain_ps")
-        nc.tensor.matmul(
-            out=gain_ps[:, 0 : 2 * HEAD], lhsT=ones[:], rhs=gain_rows[:], start=True, stop=True
-        )
         gain_sb = resident.tile([P, 2 * HEAD], F32, name="gain_sb")
-        nc.scalar.copy(out=gain_sb[:], in_=gain_ps[:, 0 : 2 * HEAD])
+
+        def spread_gains():
+            gain_ps = psum.tile([P, BANK], F32, tag="bank", name="gain_ps")
+            nc.tensor.matmul(
+                out=gain_ps[:, 0 : 2 * HEAD], lhsT=ones[:], rhs=gain_rows[:], start=True, stop=True
+            )
+            nc.scalar.copy(out=gain_sb[:], in_=gain_ps[:, 0 : 2 * HEAD])
 
         tables = []
-        for w in range(2):
+
+        def build_table(w):
             gain = gain_sb[:, w * HEAD : (w + 1) * HEAD]
             table = resident.tile([P, TOKEN_TILES, 2, HEAD], F32, name="table%d" % w)
             nc.vector.tensor_tensor(
@@ -164,9 +177,6 @@ def tile_multiheadattention_pa_kernel(
                 op1=ALU.mult,
             )
             tables.append(table)
-
-        for s in range(1, len(slabs)):
-            load_slab(s)
 
         x_codes = []
         x_scales = []
@@ -197,6 +207,10 @@ def tile_multiheadattention_pa_kernel(
             )
             x_codes.append(codes)
             x_scales.append(scales)
+            if m == 0:
+                spread_gains()
+        for w in range(2):
+            build_table(w)
 
         for s, slab in enumerate(slabs):
             for m in range(TOKEN_TILES):

@@ -29,6 +29,7 @@ SLAB = SLAB_BANKS * BANK
 SLAB_HEADS = SLAB // HEAD
 EPS = 1e-6
 NORMED_SLABS = 3
+WARM_BEFORE = 5
 HELPED_UNITS = 1
 
 FLOPS = 2 * TOKENS * D_MODEL * (2048 + 1024 + 1024)
@@ -108,10 +109,17 @@ def tile_multiheadattention_pa_kernel(
                 bank_words.append(words)
             w_words.append(bank_words)
 
-        gain_rows = resident.tile([P, 2 * HEAD], BF16, name="gain_rows")
-        nc.vector.memset(gain_rows[:], 0.0)
         ones = resident.tile([P, P], BF16, name="ones")
         nc.vector.memset(ones[:], 1.0)
+        filler = resident.tile([P, BANK], BF16, name="filler")
+        nc.vector.memset(filler[:], 0.0)
+
+        def keep_warm(count):
+            for i in range(count):
+                idle = psum.tile([P, BANK], F32, tag="bank", name="idle")
+                nc.tensor.matmul(out=idle[:], lhsT=ones[:], rhs=filler[:], start=True, stop=True)
+        gain_rows = resident.tile([P, 2 * HEAD], BF16, name="gain_rows")
+        nc.vector.memset(gain_rows[:], 0.0)
         eps = resident.tile([P, 1], F32, name="eps")
         nc.vector.memset(eps[:], EPS)
         ident = resident.tile([P, P], F32, name="ident")
@@ -180,6 +188,7 @@ def tile_multiheadattention_pa_kernel(
 
         x_codes = []
         x_scales = []
+        keep_warm(WARM_BEFORE)
         for m in range(TOKEN_TILES):
             x_pairs = x_sb[m][:].bitcast(F32)
             grouped = prep.tile([P, PASSES, P, PACK], BF16, align_bytes=64, name="grouped")
@@ -194,6 +203,7 @@ def tile_multiheadattention_pa_kernel(
                             in_=x_pairs[:, 256 * g + u : 256 * (g + 1) : 2],
                             identity=ident[:],
                         )
+                keep_warm(1)
                 nc.scalar.copy(
                     out=grouped_pairs[:, 2 * b : 2 * b + 2, :, :],
                     in_=xt[:].rearrange("p i u r -> p i r u"),

@@ -86,28 +86,29 @@ def tile_multiheadattention_pa_kernel(
             plane = resident.tile([P, PASSES, SLAB], U8, align_bytes=64, name="plane%d" % s)
             nc.vector.memset(plane[:].bitcast(I32), 0)
             w_planes.append(plane)
+            w_words.append(
+                [
+                    resident.tile([P, PASSES, 2 * BANK], U8, align_bytes=64, name="words%d_%d" % (s, b))
+                    for b in range(SLAB_BANKS)
+                ]
+            )
 
-        def load_slab(s):
-            slab = slabs[s]
-            plane = w_planes[s]
-            rows = slab["scales"].bitcast(I32).rearrange("g (j r) n -> r j g n", r=4)
-            first_word = slab["first"] // 4
+        def load_scales(s, first, width):
+            rows = slabs[s]["scales"].bitcast(I32).rearrange("g (j r) n -> r j g n", r=4)
+            first_word = (slabs[s]["first"] + first) // 4
             for r in range(4):
                 nc.sync.dma_start(
-                    out=plane[r:P:32, :, :].bitcast(I32),
-                    in_=rows[r, :, :, first_word : first_word + SLAB // 4],
+                    out=w_planes[s][r:P:32, :, first : first + width].bitcast(I32),
+                    in_=rows[r, :, :, first_word : first_word + width // 4],
                 )
 
-            source = slab["words"].bitcast(I32).rearrange("g p w -> p g w")
-            bank_words = []
-            for b in range(SLAB_BANKS):
-                words = resident.tile([P, PASSES, 2 * BANK], U8, align_bytes=64, name="words%d_%d" % (s, b))
-                first_word = (slab["first"] + b * BANK) // 2
-                nc.sync.dma_start(
-                    out=words[:].bitcast(I32), in_=source[:, :, first_word : first_word + BANK // 2]
-                )
-                bank_words.append(words)
-            w_words.append(bank_words)
+        def load_words(s, b, first_pass, passes):
+            source = slabs[s]["words"].bitcast(I32).rearrange("g p w -> p g w")
+            first_word = (slabs[s]["first"] + b * BANK) // 2
+            nc.sync.dma_start(
+                out=w_words[s][b][:, first_pass : first_pass + passes, :].bitcast(I32),
+                in_=source[:, first_pass : first_pass + passes, first_word : first_word + BANK // 2],
+            )
 
         ones = resident.tile([P, P], BF16, name="ones")
         nc.vector.memset(ones[:], 1.0)
@@ -118,13 +119,13 @@ def tile_multiheadattention_pa_kernel(
             for i in range(count):
                 idle = psum.tile([P, BANK], F32, tag="bank", name="idle")
                 nc.tensor.matmul(out=idle[:], lhsT=ones[:], rhs=filler[:], start=True, stop=True)
+
         gain_rows = resident.tile([P, 2 * HEAD], BF16, name="gain_rows")
         nc.vector.memset(gain_rows[:], 0.0)
         eps = resident.tile([P, 1], F32, name="eps")
         nc.vector.memset(eps[:], EPS)
         ident = resident.tile([P, P], F32, name="ident")
         make_identity(nc, ident[:])
-
         for s in range(len(slabs)):
             zero_plane(s)
 
@@ -139,50 +140,50 @@ def tile_multiheadattention_pa_kernel(
         nc.sync.dma_start(out=gain_rows[0:1, HEAD : 2 * HEAD], in_=k_scale.unsqueeze(0))
         for m in range(1, TOKEN_TILES):
             nc.sync.dma_start(out=x_sb[m][:], in_=x_dram[:, m, :])
-        load_slab(0)
+        load_scales(0, 0, SLAB)
+        for b in range(SLAB_BANKS):
+            load_words(0, b, 0, PASSES)
         cos_sb = resident.tile([P, TOKEN_TILES, HEAD], BF16, name="cos_sb")
         nc.sync.dma_start(out=cos_sb[:], in_=cos_dram)
         sin_sb = resident.tile([P, TOKEN_TILES, HEAD], BF16, name="sin_sb")
         nc.sync.dma_start(out=sin_sb[:], in_=sin_dram)
         for s in range(1, len(slabs)):
-            load_slab(s)
+            load_scales(s, 0, SLAB)
+            for b in range(SLAB_BANKS):
+                load_words(s, b, 0, PASSES)
 
         warm = resident.tile([P, 1], F32, name="warm")
         nc.scalar.activation(out=warm[:], in_=eps[:], func=ACT.Abs_reciprocal_sqrt)
 
-        gain_sb = resident.tile([P, 2 * HEAD], F32, name="gain_sb")
+        gain_sb = resident.tile([P, 2, 2, HALF], F32, name="gain_sb")
+        turn_sb = resident.tile([P, 2, 2, HALF], F32, name="turn_sb")
 
         def spread_gains():
             gain_ps = psum.tile([P, BANK], F32, tag="bank", name="gain_ps")
             nc.tensor.matmul(
                 out=gain_ps[:, 0 : 2 * HEAD], lhsT=ones[:], rhs=gain_rows[:], start=True, stop=True
             )
-            nc.scalar.copy(out=gain_sb[:], in_=gain_ps[:, 0 : 2 * HEAD])
+            spread = gain_ps[:, 0 : 2 * HEAD].rearrange("p (w a j) -> p w a j", w=2, a=2)
+            nc.scalar.copy(out=gain_sb[:], in_=spread)
+            nc.scalar.copy(out=turn_sb[:, :, 0, :], in_=spread[:, :, 0, :])
+            nc.scalar.mul(out=turn_sb[:, :, 1, :], in_=spread[:, :, 1, :], mul=-1.0)
 
         tables = []
 
-        def build_table(w):
-            gain = gain_sb[:, w * HEAD : (w + 1) * HEAD]
+        def build_table(w, engine):
             table = resident.tile([P, TOKEN_TILES, 2, HEAD], F32, name="table%d" % w)
-            nc.vector.tensor_tensor(
-                out=table[:, :, 0, :],
-                in0=cos_sb[:],
-                in1=gain.unsqueeze(1).to_broadcast([P, TOKEN_TILES, HEAD]),
+            shape = [P, TOKEN_TILES, 2, HALF]
+            engine.tensor_tensor(
+                out=table[:, :, 0, :].rearrange("p m (a j) -> p m a j", a=2),
+                in0=cos_sb[:].rearrange("p m (a j) -> p m a j", a=2),
+                in1=gain_sb[:, w, :, :].unsqueeze(1).to_broadcast(shape),
                 op=ALU.mult,
             )
-            nc.vector.tensor_tensor(
-                out=table[:, :, 1, 0:HALF],
-                in0=sin_sb[:, :, HALF:HEAD],
-                in1=gain[:, 0:HALF].unsqueeze(1).to_broadcast([P, TOKEN_TILES, HALF]),
+            engine.tensor_tensor(
+                out=table[:, :, 1, :].rearrange("p m (a j) -> p m a j", a=2),
+                in0=sin_sb[:].rearrange("p m (a j) -> p m a j", a=2)[:, :, ::-1, :],
+                in1=turn_sb[:, w, :, :].unsqueeze(1).to_broadcast(shape),
                 op=ALU.mult,
-            )
-            nc.vector.scalar_tensor_tensor(
-                out=table[:, :, 1, HALF:HEAD],
-                in0=sin_sb[:, :, 0:HALF],
-                scalar=-1.0,
-                in1=gain[:, HALF:HEAD].unsqueeze(1).to_broadcast([P, TOKEN_TILES, HALF]),
-                op0=ALU.mult,
-                op1=ALU.mult,
             )
             tables.append(table)
 
@@ -219,75 +220,102 @@ def tile_multiheadattention_pa_kernel(
             x_scales.append(scales)
             if m == 0:
                 spread_gains()
-        for w in range(2):
-            build_table(w)
+        build_table(0, nc.vector)
+        build_table(1, nc.vector)
 
-        for s, slab in enumerate(slabs):
-            for m in range(TOKEN_TILES):
-                banks = []
-                for b in range(SLAB_BANKS):
-                    acc = psum.tile([P, BANK], F32, tag="bank", name="acc")
-                    for g in range(PASSES):
-                        nc.tensor.matmul_mx(
-                            out=acc[:],
-                            lhsT=x_codes[m][:, g, :].bitcast(FP8X4),
-                            lhsT_scale=x_scales[m][:, g, :],
-                            rhs=w_words[s][b][:, g, :].bitcast(FP4X4),
-                            rhs_scale=w_planes[s][:, g, BANK * b : BANK * (b + 1)],
-                            start=(g == 0),
-                            stop=(g == PASSES - 1),
-                        )
-                    banks.append(acc)
+        def project(s, m, b):
+            acc = psum.tile([P, BANK], F32, tag="bank", name="acc")
+            for g in range(PASSES):
+                nc.tensor.matmul_mx(
+                    out=acc[:],
+                    lhsT=x_codes[m][:, g, :].bitcast(FP8X4),
+                    lhsT_scale=x_scales[m][:, g, :],
+                    rhs=w_words[s][b][:, g, :].bitcast(FP4X4),
+                    rhs_scale=w_planes[s][:, g, BANK * b : BANK * (b + 1)],
+                    start=(g == 0),
+                    stop=(g == PASSES - 1),
+                )
+            return acc
 
-                if slab["gain"] is None:
+        def square_sums(acc):
+            squared = squares.tile([P, BANK_HEADS, HEAD], F32, name="squared")
+            sums = small.tile([P, BANK_HEADS], F32, name="sums")
+            for h in range(BANK_HEADS):
+                nc.scalar.activation(
+                    out=squared[:, h, :],
+                    in_=acc[:, h * HEAD : (h + 1) * HEAD],
+                    func=ACT.Square,
+                    accum_out=sums[:, h : h + 1],
+                )
+            return sums
+
+        def norm_and_turn(s, m, b, acc, sums, shares):
+            inv_rms = small.tile([P, BANK_HEADS], F32, name="inv_rms")
+            nc.scalar.activation(
+                out=inv_rms[:],
+                in_=sums[:],
+                func=ACT.Abs_reciprocal_sqrt,
+                scale=1.0 / HEAD,
+                bias=eps[:],
+            )
+            for h in range(BANK_HEADS):
+                nc.vector.scalar_tensor_tensor(
+                    out=shares[:, b * BANK_HEADS + h, :, :],
+                    in0=acc[:, h * HEAD : (h + 1) * HEAD].unsqueeze(1).to_broadcast([P, 2, HEAD]),
+                    scalar=inv_rms[:, h : h + 1],
+                    in1=tables[slabs[s]["gain"]][:, m, :, :],
+                    op0=ALU.mult,
+                    op1=ALU.mult,
+                )
+
+        def add_and_store(s, m, shares):
+            slab = slabs[s]
+            result = results.tile([P, SLAB_HEADS, HEAD], F32, name="result")
+            total = result[:].rearrange("p h (a j) -> p h a j", a=2)
+            own = shares[:, :, 0, :].rearrange("p h (a j) -> p h a j", a=2)
+            other = shares[:, :, 1, :].rearrange("p h (a j) -> p h a j", a=2)[:, :, ::-1, :]
+            units_left = (NORMED_SLABS - s) * TOKEN_TILES - m
+            if units_left <= HELPED_UNITS:
+                nc.gpsimd.tensor_tensor(
+                    out=total[:, 0:BANK_HEADS], in0=own[:, 0:BANK_HEADS], in1=other[:, 0:BANK_HEADS], op=ALU.add
+                )
+                nc.vector.tensor_tensor(
+                    out=total[:, BANK_HEADS:], in0=own[:, BANK_HEADS:], in1=other[:, BANK_HEADS:], op=ALU.add
+                )
+            else:
+                nc.gpsimd.tensor_tensor(out=total, in0=own, in1=other, op=ALU.add)
+            nc.sync.dma_start(
+                out=slab["out"][:, m, slab["first"] : slab["first"] + SLAB],
+                in_=result[:].rearrange("p h j -> p (h j)"),
+            )
+
+        order = [(s, m, b) for s in range(len(slabs)) for m in range(TOKEN_TILES) for b in range(SLAB_BANKS)]
+        open_units = {}
+        waiting = []
+
+        def finish_waiting():
+            for s, m, b, acc, sums, shares in waiting:
+                norm_and_turn(s, m, b, acc, sums, shares)
+                if b == SLAB_BANKS - 1:
+                    add_and_store(s, m, shares)
+            waiting.clear()
+
+        for s, m, b in order:
+            acc = project(s, m, b)
+            if slabs[s]["gain"] is None:
+                finish_waiting()
+                if b == 0:
                     copied = copies.tile([P, SLAB], F32, name="copied")
-                    for b in range(SLAB_BANKS):
-                        nc.scalar.copy(out=copied[:, b * BANK : (b + 1) * BANK], in_=banks[b][:])
-                    nc.scalar.dma_start(out=slab["out"][:, m, :], in_=copied[:])
-                else:
+                    open_units[(s, m)] = copied
+                copied = open_units[(s, m)]
+                nc.scalar.copy(out=copied[:, b * BANK : (b + 1) * BANK], in_=acc[:])
+                if b == SLAB_BANKS - 1:
+                    nc.scalar.dma_start(out=slabs[s]["out"][:, m, :], in_=copied[:])
+            else:
+                if b == 0:
                     shares = products.tile([P, SLAB_HEADS, 2, HEAD], F32, name="shares")
-                    for b in range(SLAB_BANKS):
-                        squared = squares.tile([P, BANK_HEADS, HEAD], F32, name="squared")
-                        sums = small.tile([P, BANK_HEADS], F32, name="sums")
-                        for h in range(BANK_HEADS):
-                            nc.scalar.activation(
-                                out=squared[:, h, :],
-                                in_=banks[b][:, h * HEAD : (h + 1) * HEAD],
-                                func=ACT.Square,
-                                accum_out=sums[:, h : h + 1],
-                            )
-                        inv_rms = small.tile([P, BANK_HEADS], F32, name="inv_rms")
-                        nc.scalar.activation(
-                            out=inv_rms[:],
-                            in_=sums[:],
-                            func=ACT.Abs_reciprocal_sqrt,
-                            scale=1.0 / HEAD,
-                            bias=eps[:],
-                        )
-                        for h in range(BANK_HEADS):
-                            nc.vector.scalar_tensor_tensor(
-                                out=shares[:, b * BANK_HEADS + h, :, :],
-                                in0=banks[b][:, h * HEAD : (h + 1) * HEAD].unsqueeze(1).to_broadcast([P, 2, HEAD]),
-                                scalar=inv_rms[:, h : h + 1],
-                                in1=tables[slab["gain"]][:, m, :, :],
-                                op0=ALU.mult,
-                                op1=ALU.mult,
-                            )
-                    result = results.tile([P, SLAB_HEADS, HEAD], F32, name="result")
-                    total = result[:].rearrange("p h (a j) -> p h a j", a=2)
-                    own = shares[:, :, 0, :].rearrange("p h (a j) -> p h a j", a=2)
-                    other = shares[:, :, 1, :].rearrange("p h (a j) -> p h a j", a=2)[:, :, ::-1, :]
-                    units_left = (NORMED_SLABS - s) * TOKEN_TILES - m
-                    if units_left <= HELPED_UNITS:
-                        nc.gpsimd.tensor_tensor(
-                            out=total[:, 0:BANK_HEADS], in0=own[:, 0:BANK_HEADS], in1=other[:, 0:BANK_HEADS], op=ALU.add
-                        )
-                        nc.vector.tensor_tensor(
-                            out=total[:, BANK_HEADS:], in0=own[:, BANK_HEADS:], in1=other[:, BANK_HEADS:], op=ALU.add
-                        )
-                    else:
-                        nc.gpsimd.tensor_tensor(out=total, in0=own, in1=other, op=ALU.add)
-                    nc.sync.dma_start(
-                        out=slab["out"][:, m, slab["first"] : slab["first"] + SLAB],
-                        in_=result[:].rearrange("p h j -> p (h j)"),
-                    )
+                    open_units[(s, m)] = shares
+                shares = open_units[(s, m)]
+                sums = square_sums(acc)
+                finish_waiting()
+                waiting.append((s, m, b, acc, sums, shares))

@@ -308,9 +308,18 @@ def tile_multiheadattention_pa_kernel(
                     copied = copies.tile([P, SLAB], F32, name="copied")
                     open_units[(s, m)] = copied
                 copied = open_units[(s, m)]
-                nc.scalar.copy(out=copied[:, b * BANK : (b + 1) * BANK], in_=acc[:])
-                if b == SLAB_BANKS - 1:
-                    nc.scalar.dma_start(out=slabs[s]["out"][:, m, :], in_=copied[:])
+                if m < TOKEN_TILES - 1:
+                    nc.scalar.copy(out=copied[:, b * BANK : (b + 1) * BANK], in_=acc[:])
+                    if b == SLAB_BANKS - 1:
+                        nc.scalar.dma_start(out=slabs[s]["out"][:, m, :], in_=copied[:])
+                else:
+                    parts = 1 if b == 0 else 2
+                    for part in range(parts):
+                        first = b * BANK + part * BANK // parts
+                        columns = slice(first, first + BANK // parts)
+                        nc.scalar.copy(out=copied[:, columns], in_=acc[:, first - b * BANK : first - b * BANK + BANK // parts])
+                        queue = nc.scalar if (b == SLAB_BANKS - 1 and part == parts - 1) else nc.sync
+                        queue.dma_start(out=slabs[s]["out"][:, m, columns], in_=copied[:, columns])
             else:
                 if b == 0:
                     shares = products.tile([P, SLAB_HEADS, 2, HEAD], F32, name="shares")

@@ -155,37 +155,56 @@ def tile_multiheadattention_pa_kernel(
         warm = resident.tile([P, 1], F32, name="warm")
         nc.scalar.activation(out=warm[:], in_=eps[:], func=ACT.Abs_reciprocal_sqrt)
 
-        gain_sb = resident.tile([P, 2, 2, HALF], F32, name="gain_sb")
-        turn_sb = resident.tile([P, 2, 2, HALF], F32, name="turn_sb")
+        tables = [
+            resident.tile([P, TOKEN_TILES, 2, HEAD], F32, name="table%d" % w) for w in range(2)
+        ]
+        gain_k = resident.tile([P, 2, HALF], F32, name="gain_k")
+        turn_k = resident.tile([P, 2, HALF], F32, name="turn_k")
 
-        def spread_gains():
+        def build_tables():
             gain_ps = psum.tile([P, BANK], F32, tag="bank", name="gain_ps")
             nc.tensor.matmul(
                 out=gain_ps[:, 0 : 2 * HEAD], lhsT=ones[:], rhs=gain_rows[:], start=True, stop=True
             )
-            spread = gain_ps[:, 0 : 2 * HEAD].rearrange("p (w a j) -> p w a j", w=2, a=2)
-            nc.scalar.copy(out=gain_sb[:], in_=spread)
-            nc.scalar.copy(out=turn_sb[:, :, 0, :], in_=spread[:, :, 0, :])
-            nc.scalar.mul(out=turn_sb[:, :, 1, :], in_=spread[:, :, 1, :], mul=-1.0)
+            spread_k = gain_ps[:, HEAD : 2 * HEAD].rearrange("p (a j) -> p a j", a=2)
+            nc.scalar.copy(out=gain_k[:], in_=spread_k)
+            nc.scalar.copy(out=turn_k[:, 0, :], in_=spread_k[:, 0, :])
+            nc.scalar.mul(out=turn_k[:, 1, :], in_=spread_k[:, 1, :], mul=-1.0)
 
-        tables = []
+            nc.vector.tensor_tensor(
+                out=tables[0][:, :, 0, :],
+                in0=cos_sb[:],
+                in1=gain_ps[:, 0:HEAD].unsqueeze(1).to_broadcast([P, TOKEN_TILES, HEAD]),
+                op=ALU.mult,
+            )
+            nc.vector.tensor_tensor(
+                out=tables[0][:, :, 1, 0:HALF],
+                in0=sin_sb[:, :, HALF:HEAD],
+                in1=gain_ps[:, 0:HALF].unsqueeze(1).to_broadcast([P, TOKEN_TILES, HALF]),
+                op=ALU.mult,
+            )
+            nc.vector.scalar_tensor_tensor(
+                out=tables[0][:, :, 1, HALF:HEAD],
+                in0=sin_sb[:, :, 0:HALF],
+                scalar=-1.0,
+                in1=gain_ps[:, HALF:HEAD].unsqueeze(1).to_broadcast([P, TOKEN_TILES, HALF]),
+                op0=ALU.mult,
+                op1=ALU.mult,
+            )
 
-        def build_table(w, engine):
-            table = resident.tile([P, TOKEN_TILES, 2, HEAD], F32, name="table%d" % w)
             shape = [P, TOKEN_TILES, 2, HALF]
-            engine.tensor_tensor(
-                out=table[:, :, 0, :].rearrange("p m (a j) -> p m a j", a=2),
+            nc.gpsimd.tensor_tensor(
+                out=tables[1][:, :, 0, :].rearrange("p m (a j) -> p m a j", a=2),
                 in0=cos_sb[:].rearrange("p m (a j) -> p m a j", a=2),
-                in1=gain_sb[:, w, :, :].unsqueeze(1).to_broadcast(shape),
+                in1=gain_k[:].unsqueeze(1).to_broadcast(shape),
                 op=ALU.mult,
             )
-            engine.tensor_tensor(
-                out=table[:, :, 1, :].rearrange("p m (a j) -> p m a j", a=2),
+            nc.gpsimd.tensor_tensor(
+                out=tables[1][:, :, 1, :].rearrange("p m (a j) -> p m a j", a=2),
                 in0=sin_sb[:].rearrange("p m (a j) -> p m a j", a=2)[:, :, ::-1, :],
-                in1=turn_sb[:, w, :, :].unsqueeze(1).to_broadcast(shape),
+                in1=turn_k[:].unsqueeze(1).to_broadcast(shape),
                 op=ALU.mult,
             )
-            tables.append(table)
 
         x_codes = []
         x_scales = []
@@ -218,10 +237,7 @@ def tile_multiheadattention_pa_kernel(
             )
             x_codes.append(codes)
             x_scales.append(scales)
-            if m == 0:
-                spread_gains()
-        build_table(0, nc.vector)
-        build_table(1, nc.vector)
+        build_tables()
 
         def project(s, m, b):
             acc = psum.tile([P, BANK], F32, tag="bank", name="acc")

@@ -30,6 +30,8 @@ SLAB_HEADS = SLAB // HEAD
 EPS = 1e-6
 NORMED_SLABS = 3
 WARM_BEFORE = 5
+WARM_TILES = 2
+WARM_EACH = 2
 HELPED_UNITS = 1
 
 FLOPS = 2 * TOKENS * D_MODEL * (2048 + 1024 + 1024)
@@ -141,8 +143,9 @@ def tile_multiheadattention_pa_kernel(
         for m in range(1, TOKEN_TILES):
             nc.sync.dma_start(out=x_sb[m][:], in_=x_dram[:, m, :])
         load_scales(0, 0, SLAB)
-        for b in range(SLAB_BANKS):
-            load_words(0, b, 0, PASSES)
+        load_words(0, 0, 0, PASSES // 2)
+        load_words(0, 0, PASSES // 2, PASSES // 2)
+        load_words(0, 1, 0, PASSES)
         cos_sb = resident.tile([P, TOKEN_TILES, HEAD], BF16, name="cos_sb")
         nc.sync.dma_start(out=cos_sb[:], in_=cos_dram)
         sin_sb = resident.tile([P, TOKEN_TILES, HEAD], BF16, name="sin_sb")
@@ -223,11 +226,12 @@ def tile_multiheadattention_pa_kernel(
                             in_=x_pairs[:, 256 * g + u : 256 * (g + 1) : 2],
                             identity=ident[:],
                         )
-                keep_warm(1)
                 nc.scalar.copy(
                     out=grouped_pairs[:, 2 * b : 2 * b + 2, :, :],
                     in_=xt[:].rearrange("p i u r -> p i r u"),
                 )
+            if m >= TOKEN_TILES - WARM_TILES:
+                keep_warm(WARM_EACH)
             codes = resident.tile([P, PASSES, P], U32, align_bytes=64, name="x_codes%d" % m)
             scales = resident.tile([P, PASSES, P], U8, align_bytes=64, name="x_scales%d" % m)
             nc.vector.quantize_mx(

@@ -32,6 +32,9 @@ NORMED_SLABS = 3
 WARM_BEFORE = 5
 WARM_TILES = 2
 WARM_EACH = 2
+PLANE_SHIFT = 128
+CODES_SHIFT = 64
+SCALES_SHIFT = 192
 HELPED_UNITS = 1
 
 FLOPS = 2 * TOKENS * D_MODEL * (2048 + 1024 + 1024)
@@ -85,12 +88,12 @@ def tile_multiheadattention_pa_kernel(
         w_planes = []
 
         def zero_plane(s):
-            plane = resident.tile([P, PASSES, SLAB], U8, align_bytes=64, name="plane%d" % s)
-            nc.vector.memset(plane[:].bitcast(I32), 0)
-            w_planes.append(plane)
+            whole = resident.tile([P, PLANE_SHIFT + PASSES * SLAB], U8, align_bytes=256, name="plane%d" % s)
+            nc.vector.memset(whole[:].bitcast(I32), 0)
+            w_planes.append(whole[:, PLANE_SHIFT:].rearrange("p (g n) -> p g n", g=PASSES))
             w_words.append(
                 [
-                    resident.tile([P, PASSES, 2 * BANK], U8, align_bytes=64, name="words%d_%d" % (s, b))
+                    resident.tile([P, PASSES, 2 * BANK], U8, align_bytes=256, name="words%d_%d" % (s, b))
                     for b in range(SLAB_BANKS)
                 ]
             )
@@ -232,15 +235,15 @@ def tile_multiheadattention_pa_kernel(
                 )
             if m >= TOKEN_TILES - WARM_TILES:
                 keep_warm(WARM_EACH)
-            codes = resident.tile([P, PASSES, P], U32, align_bytes=64, name="x_codes%d" % m)
-            scales = resident.tile([P, PASSES, P], U8, align_bytes=64, name="x_scales%d" % m)
+            codes = resident.tile([P, CODES_SHIFT // 4 + PASSES * P], U32, align_bytes=256, name="x_codes%d" % m)
+            scales = resident.tile([P, SCALES_SHIFT + PASSES * P], U8, align_bytes=256, name="x_scales%d" % m)
             nc.vector.quantize_mx(
-                out=codes[:].rearrange("p g r -> p (g r)").bitcast(FP8X4),
-                scales=scales[:].rearrange("p g r -> p (g r)"),
+                out=codes[:, CODES_SHIFT // 4 :].bitcast(FP8X4),
+                scales=scales[:, SCALES_SHIFT:],
                 in_=grouped[:].rearrange("p g r t -> p (g r t)"),
             )
-            x_codes.append(codes)
-            x_scales.append(scales)
+            x_codes.append(codes[:, CODES_SHIFT // 4 :].rearrange("p (g r) -> p g r", g=PASSES))
+            x_scales.append(scales[:, SCALES_SHIFT:].rearrange("p (g r) -> p g r", g=PASSES))
         build_tables()
 
         def project(s, m, b):

from contextlib import ExitStack

import concourse.mybir as mybir
from concourse.masks import make_identity

F32 = mybir.dt.float32
BF16 = mybir.dt.bfloat16
I32 = mybir.dt.int32
U32 = mybir.dt.uint32
U8 = mybir.dt.uint8
FP8X4 = mybir.dt.float8_e4m3fn_x4
FP4X4 = mybir.dt.float4_e2m1fn_x4
ALU = mybir.AluOpType
ACT = mybir.ActivationFunctionType

P = 128
TOKENS = 512
TOKEN_TILES = TOKENS // P
D_MODEL = 2048
PACK = 4
K_PASS = P * PACK
PASSES = D_MODEL // K_PASS
HEAD = 128
HALF = HEAD // 2
BANK = 512
BANK_HEADS = BANK // HEAD
SLAB_BANKS = 2
SLAB = SLAB_BANKS * BANK
SLAB_HEADS = SLAB // HEAD
EPS = 1e-6
NORMED_SLABS = 3
WARM_BEFORE = 5
WARM_TILES = 2
WARM_EACH = 2
PLANE_SHIFT = 128
CODES_SHIFT = 64
SCALES_SHIFT = 192
HELPED_UNITS = 1

FLOPS = 2 * TOKENS * D_MODEL * (2048 + 1024 + 1024)


def tile_multiheadattention_pa_kernel(
    tc,
    hidden_states,
    cos,
    sin,
    Wq_words,
    Wq_scales,
    Wk_words,
    Wk_scales,
    Wv_words,
    Wv_scales,
    q_scale,
    k_scale,
    out_0,
    out_1,
    out_2,
):
    nc = tc.nc

    x_dram = hidden_states[0].rearrange("(p m) d -> p m d", m=TOKEN_TILES)
    cos_dram = cos[0].rearrange("(p m) j -> p m j", m=TOKEN_TILES)
    sin_dram = sin[0].rearrange("(p m) j -> p m j", m=TOKEN_TILES)
    q_dram = out_0[0].rearrange("(p m) h j -> p m (h j)", m=TOKEN_TILES)
    k_dram = out_1[0].rearrange("(p m) h j -> p m (h j)", m=TOKEN_TILES)
    v_dram = out_2[0].rearrange("(p m) h j -> p m (h j)", m=TOKEN_TILES)

    slabs = (
        {"words": Wq_words, "scales": Wq_scales, "first": 0, "out": q_dram, "gain": 0},
        {"words": Wq_words, "scales": Wq_scales, "first": SLAB, "out": q_dram, "gain": 0},
        {"words": Wk_words, "scales": Wk_scales, "first": 0, "out": k_dram, "gain": 1},
        {"words": Wv_words, "scales": Wv_scales, "first": 0, "out": v_dram, "gain": None},
    )

    with ExitStack() as ctx:
        ctx.enter_context(tc.manual_schedule())
        resident = ctx.enter_context(tc.tile_pool(name="resident", bufs=1))
        prep = ctx.enter_context(tc.tile_pool(name="prep", bufs=4))
        small = ctx.enter_context(tc.tile_pool(name="small", bufs=6))
        squares = ctx.enter_context(tc.tile_pool(name="squares", bufs=3))
        products = ctx.enter_context(tc.tile_pool(name="products", bufs=6))
        results = ctx.enter_context(tc.tile_pool(name="results", bufs=6))
        copies = ctx.enter_context(tc.tile_pool(name="copies", bufs=4))
        psum = ctx.enter_context(tc.psum_pool(name="psum", bufs=8))

        w_words = []
        w_planes = []

        def zero_plane(s):
            whole = resident.tile([P, PLANE_SHIFT + PASSES * SLAB], U8, align_bytes=256, name="plane%d" % s)
            nc.vector.memset(whole[:].bitcast(I32), 0)
            w_planes.append(whole[:, PLANE_SHIFT:].rearrange("p (g n) -> p g n", g=PASSES))
            w_words.append(
                [
                    resident.tile([P, PASSES, 2 * BANK], U8, align_bytes=256, name="words%d_%d" % (s, b))
                    for b in range(SLAB_BANKS)
                ]
            )

        def load_scales(s, first, width):
            rows = slabs[s]["scales"].bitcast(I32).rearrange("g (j r) n -> r j g n", r=4)
            first_word = (slabs[s]["first"] + first) // 4
            for r in range(4):
                nc.sync.dma_start(
                    out=w_planes[s][r:P:32, :, first : first + width].bitcast(I32),
                    in_=rows[r, :, :, first_word : first_word + width // 4],
                )

        def load_words(s, b, first_pass, passes):
            source = slabs[s]["words"].bitcast(I32).rearrange("g p w -> p g w")
            first_word = (slabs[s]["first"] + b * BANK) // 2
            nc.sync.dma_start(
                out=w_words[s][b][:, first_pass : first_pass + passes, :].bitcast(I32),
                in_=source[:, first_pass : first_pass + passes, first_word : first_word + BANK // 2],
            )

        ones = resident.tile([P, P], BF16, name="ones")
        nc.vector.memset(ones[:], 1.0)
        filler = resident.tile([P, BANK], BF16, name="filler")
        nc.vector.memset(filler[:], 0.0)

        def keep_warm(count):
            for i in range(count):
                idle = psum.tile([P, BANK], F32, tag="bank", name="idle")
                nc.tensor.matmul(out=idle[:], lhsT=ones[:], rhs=filler[:], start=True, stop=True)

        gain_rows = resident.tile([P, 2 * HEAD], BF16, name="gain_rows")
        nc.vector.memset(gain_rows[:], 0.0)
        eps = resident.tile([P, 1], F32, name="eps")
        nc.vector.memset(eps[:], EPS)
        ident = resident.tile([P, P], F32, name="ident")
        make_identity(nc, ident[:])
        for s in range(len(slabs)):
            zero_plane(s)

        x_sb = []
        for m in range(TOKEN_TILES):
            x_tile = resident.tile([P, D_MODEL], BF16, name="x%d" % m)
            x_sb.append(x_tile)
        for half in range(2):
            columns = slice(half * D_MODEL // 2, (half + 1) * D_MODEL // 2)
            nc.sync.dma_start(out=x_sb[0][:, columns], in_=x_dram[:, 0, columns])
        nc.sync.dma_start(out=gain_rows[0:1, 0:HEAD], in_=q_scale.unsqueeze(0))
        nc.sync.dma_start(out=gain_rows[0:1, HEAD : 2 * HEAD], in_=k_scale.unsqueeze(0))
        for m in range(1, TOKEN_TILES):
            nc.sync.dma_start(out=x_sb[m][:], in_=x_dram[:, m, :])
        load_scales(0, 0, SLAB)
        load_words(0, 0, 0, PASSES // 2)
        load_words(0, 0, PASSES // 2, PASSES // 2)
        load_words(0, 1, 0, PASSES)
        cos_sb = resident.tile([P, TOKEN_TILES, HEAD], BF16, name="cos_sb")
        nc.sync.dma_start(out=cos_sb[:], in_=cos_dram)
        sin_sb = resident.tile([P, TOKEN_TILES, HEAD], BF16, name="sin_sb")
        nc.sync.dma_start(out=sin_sb[:], in_=sin_dram)
        for s in range(1, len(slabs)):
            load_scales(s, 0, SLAB)
            for b in range(SLAB_BANKS):
                load_words(s, b, 0, PASSES)

        warm = resident.tile([P, 1], F32, name="warm")
        nc.scalar.activation(out=warm[:], in_=eps[:], func=ACT.Abs_reciprocal_sqrt)

        tables = [
            resident.tile([P, TOKEN_TILES, 2, HEAD], F32, name="table%d" % w) for w in range(2)
        ]
        gain_k = resident.tile([P, 2, HALF], F32, name="gain_k")
        turn_k = resident.tile([P, 2, HALF], F32, name="turn_k")

        def build_tables():
            gain_ps = psum.tile([P, BANK], F32, tag="bank", name="gain_ps")
            nc.tensor.matmul(
                out=gain_ps[:, 0 : 2 * HEAD], lhsT=ones[:], rhs=gain_rows[:], start=True, stop=True
            )
            spread_k = gain_ps[:, HEAD : 2 * HEAD].rearrange("p (a j) -> p a j", a=2)
            nc.scalar.copy(out=gain_k[:], in_=spread_k)
            nc.scalar.copy(out=turn_k[:, 0, :], in_=spread_k[:, 0, :])
            nc.scalar.mul(out=turn_k[:, 1, :], in_=spread_k[:, 1, :], mul=-1.0)

            nc.vector.tensor_tensor(
                out=tables[0][:, :, 0, :],
                in0=cos_sb[:],
                in1=gain_ps[:, 0:HEAD].unsqueeze(1).to_broadcast([P, TOKEN_TILES, HEAD]),
                op=ALU.mult,
            )
            nc.vector.tensor_tensor(
                out=tables[0][:, :, 1, 0:HALF],
                in0=sin_sb[:, :, HALF:HEAD],
                in1=gain_ps[:, 0:HALF].unsqueeze(1).to_broadcast([P, TOKEN_TILES, HALF]),
                op=ALU.mult,
            )
            nc.vector.scalar_tensor_tensor(
                out=tables[0][:, :, 1, HALF:HEAD],
                in0=sin_sb[:, :, 0:HALF],
                scalar=-1.0,
                in1=gain_ps[:, HALF:HEAD].unsqueeze(1).to_broadcast([P, TOKEN_TILES, HALF]),
                op0=ALU.mult,
                op1=ALU.mult,
            )

            shape = [P, TOKEN_TILES, 2, HALF]
            nc.gpsimd.tensor_tensor(
                out=tables[1][:, :, 0, :].rearrange("p m (a j) -> p m a j", a=2),
                in0=cos_sb[:].rearrange("p m (a j) -> p m a j", a=2),
                in1=gain_k[:].unsqueeze(1).to_broadcast(shape),
                op=ALU.mult,
            )
            nc.gpsimd.tensor_tensor(
                out=tables[1][:, :, 1, :].rearrange("p m (a j) -> p m a j", a=2),
                in0=sin_sb[:].rearrange("p m (a j) -> p m a j", a=2)[:, :, ::-1, :],
                in1=turn_k[:].unsqueeze(1).to_broadcast(shape),
                op=ALU.mult,
            )

        x_codes = []
        x_scales = []
        keep_warm(WARM_BEFORE)
        for m in range(TOKEN_TILES):
            x_pairs = x_sb[m][:].bitcast(F32)
            grouped = prep.tile([P, PASSES, P, PACK], BF16, align_bytes=64, name="grouped")
            grouped_pairs = grouped[:].bitcast(F32)
            for b in range(2):
                xt = psum.tile([P, 2, 2, P], F32, tag="bank", name="xt")
                for i in range(2):
                    g = 2 * b + i
                    for u in range(2):
                        nc.tensor.transpose(
                            out=xt[:, i, u, :],
                            in_=x_pairs[:, 256 * g + u : 256 * (g + 1) : 2],
                            identity=ident[:],
                        )
                nc.scalar.copy(
                    out=grouped_pairs[:, 2 * b : 2 * b + 2, :, :],
                    in_=xt[:].rearrange("p i u r -> p i r u"),
                )
            if m >= TOKEN_TILES - WARM_TILES:
                keep_warm(WARM_EACH)
            codes = resident.tile([P, CODES_SHIFT // 4 + PASSES * P], U32, align_bytes=256, name="x_codes%d" % m)
            scales = resident.tile([P, SCALES_SHIFT + PASSES * P], U8, align_bytes=256, name="x_scales%d" % m)
            nc.vector.quantize_mx(
                out=codes[:, CODES_SHIFT // 4 :].bitcast(FP8X4),
                scales=scales[:, SCALES_SHIFT:],
                in_=grouped[:].rearrange("p g r t -> p (g r t)"),
            )
            x_codes.append(codes[:, CODES_SHIFT // 4 :].rearrange("p (g r) -> p g r", g=PASSES))
            x_scales.append(scales[:, SCALES_SHIFT:].rearrange("p (g r) -> p g r", g=PASSES))
        build_tables()

        def project(s, m, b):
            acc = psum.tile([P, BANK], F32, tag="bank", name="acc")
            for g in range(PASSES):
                nc.tensor.matmul_mx(
                    out=acc[:],
                    lhsT=x_codes[m][:, g, :].bitcast(FP8X4),
                    lhsT_scale=x_scales[m][:, g, :],
                    rhs=w_words[s][b][:, g, :].bitcast(FP4X4),
                    rhs_scale=w_planes[s][:, g, BANK * b : BANK * (b + 1)],
                    start=(g == 0),
                    stop=(g == PASSES - 1),
                )
            return acc

        def square_sums(acc):
            squared = squares.tile([P, BANK_HEADS, HEAD], F32, name="squared")
            sums = small.tile([P, BANK_HEADS], F32, name="sums")
            for h in range(BANK_HEADS):
                nc.scalar.activation(
                    out=squared[:, h, :],
                    in_=acc[:, h * HEAD : (h + 1) * HEAD],
                    func=ACT.Square,
                    accum_out=sums[:, h : h + 1],
                )
            return sums

        def norm_and_turn(s, m, b, acc, sums, shares):
            inv_rms = small.tile([P, BANK_HEADS], F32, name="inv_rms")
            nc.scalar.activation(
                out=inv_rms[:],
                in_=sums[:],
                func=ACT.Abs_reciprocal_sqrt,
                scale=1.0 / HEAD,
                bias=eps[:],
            )
            for h in range(BANK_HEADS):
                nc.vector.scalar_tensor_tensor(
                    out=shares[:, b * BANK_HEADS + h, :, :],
                    in0=acc[:, h * HEAD : (h + 1) * HEAD].unsqueeze(1).to_broadcast([P, 2, HEAD]),
                    scalar=inv_rms[:, h : h + 1],
                    in1=tables[slabs[s]["gain"]][:, m, :, :],
                    op0=ALU.mult,
                    op1=ALU.mult,
                )

        def add_and_store(s, m, shares):
            slab = slabs[s]
            result = results.tile([P, SLAB_HEADS, HEAD], F32, name="result")
            total = result[:].rearrange("p h (a j) -> p h a j", a=2)
            own = shares[:, :, 0, :].rearrange("p h (a j) -> p h a j", a=2)
            other = shares[:, :, 1, :].rearrange("p h (a j) -> p h a j", a=2)[:, :, ::-1, :]
            units_left = (NORMED_SLABS - s) * TOKEN_TILES - m
            if units_left <= HELPED_UNITS:
                nc.gpsimd.tensor_tensor(
                    out=total[:, 0:BANK_HEADS], in0=own[:, 0:BANK_HEADS], in1=other[:, 0:BANK_HEADS], op=ALU.add
                )
                nc.vector.tensor_tensor(
                    out=total[:, BANK_HEADS:], in0=own[:, BANK_HEADS:], in1=other[:, BANK_HEADS:], op=ALU.add
                )
            else:
                nc.gpsimd.tensor_tensor(out=total, in0=own, in1=other, op=ALU.add)
            nc.sync.dma_start(
                out=slab["out"][:, m, slab["first"] : slab["first"] + SLAB],
                in_=result[:].rearrange("p h j -> p (h j)"),
            )

        order = [(s, m, b) for s in range(len(slabs)) for m in range(TOKEN_TILES) for b in range(SLAB_BANKS)]
        open_units = {}
        waiting = []

        def finish_waiting():
            for s, m, b, acc, sums, shares in waiting:
                norm_and_turn(s, m, b, acc, sums, shares)
                if b == SLAB_BANKS - 1:
                    add_and_store(s, m, shares)
            waiting.clear()

        for s, m, b in order:
            acc = project(s, m, b)
            if slabs[s]["gain"] is None:
                finish_waiting()
                if b == 0:
                    copied = copies.tile([P, SLAB], F32, name="copied")
                    open_units[(s, m)] = copied
                copied = open_units[(s, m)]
                if m < TOKEN_TILES - 1:
                    nc.scalar.copy(out=copied[:, b * BANK : (b + 1) * BANK], in_=acc[:])
                    if b == SLAB_BANKS - 1:
                        nc.scalar.dma_start(out=slabs[s]["out"][:, m, :], in_=copied[:])
                else:
                    parts = 1 if b == 0 else 2
                    for part in range(parts):
                        first = b * BANK + part * BANK // parts
                        columns = slice(first, first + BANK // parts)
                        nc.scalar.copy(out=copied[:, columns], in_=acc[:, first - b * BANK : first - b * BANK + BANK // parts])
                        queue = nc.scalar if (b == SLAB_BANKS - 1 and part == parts - 1) else nc.sync
                        queue.dma_start(out=slabs[s]["out"][:, m, columns], in_=copied[:, columns])
            else:
                if b == 0:
                    shares = products.tile([P, SLAB_HEADS, 2, HEAD], F32, name="shares")
                    open_units[(s, m)] = shares
                shares = open_units[(s, m)]
                sums = square_sums(acc)
                finish_waiting()
                waiting.append((s, m, b, acc, sums, shares))
